import numpy as np
import ml_dtypes


def mxq(x, axis, fmt="e4m3"):
    dtype, down = {"e4m3": (ml_dtypes.float8_e4m3fn, 7), "e5m2": (ml_dtypes.float8_e5m2, 14)}[fmt]
    v = np.moveaxis(np.asarray(x, np.float32).astype(ml_dtypes.bfloat16).astype(np.float64), axis, -1)
    blocks = v.reshape(v.shape[:-1] + (-1, 32))
    amax = np.abs(blocks).max(-1, keepdims=True)
    byte = np.maximum(np.where(amax > 0, np.frexp(amax)[1] - 1 + 127, 0) - down, 1)
    scale = np.exp2(byte - 127.0)
    codes = (blocks / scale).astype(np.float32).astype(dtype).astype(np.float64)
    return np.moveaxis((codes * scale).reshape(v.shape), -1, axis)


WIDE = False


def mx_kscale(k):
    if not WIDE:
        return np.ones(k)
    levels = np.array([10, -10, 5, -5, 0])
    if k % 512:
        return np.exp2(np.random.permutation(np.resize(levels, k // 32))).repeat(32)
    a = np.empty((k // 512, 16))
    for p in range(k // 512):
        a[p, :8] = np.random.permutation(np.resize(levels, 8))
        for g in range(8):
            far = levels[np.abs(levels - a[p, g]) >= 10]
            a[p, g + 8] = far[np.random.randint(len(far))]
    return np.exp2(a.ravel()).repeat(32)


BF16 = ml_dtypes.bfloat16


def bf(x):
    return np.asarray(x, np.float32).astype(BF16)


def f64(x):
    return np.asarray(x).astype(np.float64)


B, T, E, V, NH, C = 2, 2048, 512, 2048, 4, 512
KD = E // NH
SCALING = KD ** -0.5


def rotate_every_two(x):
    x1 = x[..., 0::2]
    x2 = x[..., 1::2]
    return np.stack((-x2, x1), axis=-1).reshape(x.shape)


def theta_shift(x, sin, cos):
    return x * cos + rotate_every_two(x) * sin


def rope_tables():
    half = np.arange(0, KD, 2) / KD
    angle = np.repeat(1.0 / 10000.0 ** half, 2)
    pos = np.arange(T)
    return np.sin(pos[:, None] * angle[None, :]), np.cos(pos[:, None] * angle[None, :])


def setup_inputs():
    s = mx_kscale(E)
    sin, cos = rope_tables()
    return {"hidden_states": bf(np.random.standard_normal((B, T, E)) * s),
            "wq": bf(np.random.standard_normal((E, E)) / np.sqrt(E) / s[None, :]),
            "wk": bf(np.random.standard_normal((E, E)) * 2.0 / np.sqrt(E) / s[None, :]),
            "sin": bf(sin), "cos": bf(cos)}


def reference(hidden_states, wq, wk, sin, cos):
    xq = mxq(f64(hidden_states), 2, "e4m3")
    q = xq @ mxq(f64(wq), 1, "e4m3").T
    k = xq @ mxq(f64(wk), 1, "e4m3").T
    q = q.reshape(B, T, NH, KD).transpose(0, 2, 1, 3)
    k = k.reshape(B, T, NH, KD).transpose(0, 2, 1, 3) * SCALING
    return theta_shift(q, f64(sin), f64(cos)), theta_shift(k, f64(sin), f64(cos))

@@ -1,0 +1,209 @@
+import concourse.mybir as mybir
+from concourse.masks import make_identity
+
+F32 = mybir.dt.float32
+BF16 = mybir.dt.bfloat16
+U32 = mybir.dt.uint32
+U8 = mybir.dt.uint8
+FP8X4 = mybir.dt.float8_e4m3fn_x4
+MULT = mybir.AluOpType.mult
+ADD = mybir.AluOpType.add
+
+P = 128
+BATCH, SEQ, EMBED, HEADS = 2, 2048, 512, 4
+HEAD_DIM = EMBED // HEADS
+K_FACTOR = HEAD_DIM**-0.5
+PACK = 4
+WORDS = EMBED // 2
+BANK = 512
+BANK_BLOCKS = BANK // WORDS
+CHUNK_BLOCKS = 4
+CHUNK = CHUNK_BLOCKS * P
+CHUNKS_PER_BATCH = SEQ // CHUNK
+CHUNKS = BATCH * CHUNKS_PER_BATCH
+PIECE_BLOCKS = 2
+PIECES = CHUNK_BLOCKS // PIECE_BLOCKS
+VECTOR_ADDITIONS = 1
+
+FLOPS = 2 * BATCH * SEQ * EMBED * 2 * EMBED
+
+
+def tile_nucleusxmultiscaleretention_pa_t_kernel(
+    tc, hidden_states, wq, wk, sin, cos, out_0, out_1
+):
+    nc = tc.nc
+    with (
+        tc.tile_pool(name="keep", bufs=1) as keep,
+        tc.tile_pool(name="tokens", bufs=CHUNKS) as tokens,
+        tc.tile_pool(name="regroup", bufs=2) as regroup,
+        tc.tile_pool(name="quantised", bufs=2) as quantised,
+        tc.tile_pool(name="results", bufs=6) as results,
+        tc.tile_pool(name="products", bufs=4) as products,
+        tc.psum_pool(name="flipped", bufs=2) as flipped,
+        tc.psum_pool(name="sums", bufs=3) as sums,
+    ):
+        identity = keep.tile([P, P], F32)
+        make_identity(nc, identity[:])
+        pair_swap = keep.tile([P, P], F32)
+        identity_pairs = identity[:].rearrange("p (j two) -> p j two", two=2)
+        pair_swap_pairs = pair_swap[:].rearrange("p (j two) -> p j two", two=2)
+        nc.vector.tensor_copy(out=pair_swap_pairs[:, :, 0:1], in_=identity_pairs[:, :, 1:2])
+        nc.vector.tensor_copy(out=pair_swap_pairs[:, :, 1:2], in_=identity_pairs[:, :, 0:1])
+
+        def load_weight(w, tag):
+            rows = keep.tile([P, HEADS * EMBED], BF16, name=tag + "_rows")
+            nc.sync.dma_start(
+                out=rows[:].rearrange("p (h k) -> p h k", h=HEADS),
+                in_=w.rearrange("(h p) k -> p h k", p=P),
+            )
+            return rows
+
+        def load_tokens(chunk):
+            b, place = divmod(chunk, CHUNKS_PER_BATCH)
+            rows = tokens.tile([P, CHUNK_BLOCKS * EMBED], BF16, name="token_rows")
+            nc.sync.dma_start(
+                out=rows[:],
+                in_=hidden_states[b, place * CHUNK : (place + 1) * CHUNK, :].rearrange(
+                    "(p i) k -> p (i k)", i=CHUNK_BLOCKS
+                ),
+            )
+            return rows
+
+        def load_table(table, tag):
+            rows = keep.tile([P, CHUNKS_PER_BATCH, CHUNK_BLOCKS, HEAD_DIM], BF16, name=tag)
+            nc.sync.dma_start(
+                out=rows[:].rearrange("p c i d -> p c (i d)"),
+                in_=table.rearrange("(c p i) d -> p c (i d)", p=P, i=CHUNK_BLOCKS),
+            )
+            return rows
+
+        wq_rows = load_weight(wq, "wq")
+        token_rows = [load_tokens(0)]
+        cos_table = load_table(cos, "cos_table")
+        sin_signed = load_table(sin, "sin_signed")
+        wk_rows = load_weight(wk, "wk")
+        for chunk in range(1, CHUNKS):
+            token_rows.append(load_tokens(chunk))
+
+        def regroup_rows(rows, permutation, grouped_words, vector_helps):
+            words = rows[:].bitcast(F32)
+            for first in range(0, rows.shape[1] // EMBED, BANK_BLOCKS):
+                bank = flipped.tile([P, BANK], F32)
+                for j in range(BANK_BLOCKS):
+                    for u in range(2):
+                        nc.tensor.transpose(
+                            bank[:, (2 * j + u) * P : (2 * j + u + 1) * P],
+                            words[:, (first + j) * WORDS + u : (first + j + 1) * WORDS : 2],
+                            permutation[:],
+                        )
+                dense = grouped_words[:, first : first + BANK_BLOCKS]
+                hopping = bank[:].rearrange("p (j u r) -> p j r u", j=BANK_BLOCKS, u=2)
+                if vector_helps and first % (2 * BANK_BLOCKS) > 0:
+                    nc.vector.tensor_copy(out=dense, in_=hopping)
+                else:
+                    nc.scalar.copy(out=dense, in_=hopping)
+
+        def as_words(grouped):
+            return grouped[:].bitcast(F32).rearrange("p (j r u) -> p j r u", r=P, u=2)
+
+        def regroup_weight(rows):
+            grouped_weight = regroup.tile([P, 2 * EMBED * PACK], BF16, align_bytes=64)
+            regroup_rows(rows, identity, as_words(grouped_weight)[:, 0:HEADS], True)
+            regroup_rows(rows, pair_swap, as_words(grouped_weight)[:, HEADS : 2 * HEADS], True)
+            return grouped_weight
+
+        def regroup_tokens(rows, vector_helps):
+            grouped_tokens = regroup.tile([P, CHUNK * PACK], BF16, align_bytes=64)
+            regroup_rows(rows, identity, as_words(grouped_tokens), vector_helps)
+            return grouped_tokens
+
+        def quantise(grouped, pool, tag):
+            columns = grouped.shape[1] // PACK
+            codes = pool.tile([P, columns], U32, name=tag + "_codes", align_bytes=64)
+            scales = pool.tile([P, columns], U8, name=tag + "_scales", align_bytes=64)
+            nc.vector.quantize_mx(out=codes[:].bitcast(FP8X4), scales=scales[:], in_=grouped[:])
+            return codes, scales
+
+        def project_and_rotate(chunk, piece, token_operand, weight_operand, factor, out, adder):
+            b, place = divmod(chunk, CHUNKS_PER_BATCH)
+            token_codes, token_scales = token_operand
+            weight_codes, weight_scales = weight_operand
+            rotated = results.tile([P, HEADS, PIECE_BLOCKS, HEAD_DIM], F32)
+            turned = products.tile([P, HEADS, PIECE_BLOCKS, HEAD_DIM], F32)
+            for j in range(PIECE_BLOCKS):
+                i = piece * PIECE_BLOCKS + j
+                block = slice(i * P, (i + 1) * P)
+                straight = sums.tile([P, BANK], F32)
+                swapped = sums.tile([P, BANK], F32)
+                for version, bank in enumerate((straight, swapped)):
+                    features = slice(version * EMBED, (version + 1) * EMBED)
+                    nc.tensor.matmul_mx(
+                        out=bank[:],
+                        lhsT=token_codes[:, block].bitcast(FP8X4),
+                        lhsT_scale=token_scales[:, block],
+                        rhs=weight_codes[:, features].bitcast(FP8X4),
+                        rhs_scale=weight_scales[:, features],
+                        start=True,
+                        stop=True,
+                    )
+                for bank, table, product in (
+                    (straight, cos_table, rotated),
+                    (swapped, sin_signed, turned),
+                ):
+                    nc.vector.scalar_tensor_tensor(
+                        out=product[:, :, j, :],
+                        in0=bank[:].rearrange("p (h d) -> p h d", h=HEADS),
+                        scalar=factor,
+                        in1=table[:, place, i, :].unsqueeze(1).to_broadcast([P, HEADS, HEAD_DIM]),
+                        op0=MULT,
+                        op1=MULT,
+                    )
+            adder.tensor_tensor(out=rotated[:], in0=rotated[:], in1=turned[:], op=ADD)
+            out_rows = out[b, :, place * CHUNK : (place + 1) * CHUNK, :].rearrange(
+                "h (p i) d -> p h i d", i=CHUNK_BLOCKS
+            )
+            blocks = slice(piece * PIECE_BLOCKS, (piece + 1) * PIECE_BLOCKS)
+            nc.sync.dma_start(
+                out=out_rows[:, :, blocks, :].rearrange("p h i d -> p h (i d)"),
+                in_=rotated[:].rearrange("p h i d -> p h (i d)"),
+            )
+
+        def negate_even_features(place):
+            even = sin_signed[:, place].rearrange("p i (j two) -> p (i j) two", two=2)[:, :, 0:1]
+            nc.scalar.mul(out=even, in_=even, mul=-1.0)
+
+        def adder_of(chunk, step):
+            additions_left = (CHUNKS - chunk) * 2 * PIECES - step
+            return nc.vector if additions_left <= VECTOR_ADDITIONS else nc.gpsimd
+
+        with tc.manual_schedule():
+            wq_operand = quantise(regroup_weight(wq_rows), keep, "wq")
+            token_operand = quantise(regroup_tokens(token_rows[0], True), quantised, "token")
+            for chunk in range(CHUNKS):
+                first_chunk = chunk == 0
+                last_chunk = chunk == CHUNKS - 1
+                if chunk < CHUNKS_PER_BATCH:
+                    negate_even_features(chunk)
+                for piece in range(PIECES):
+                    project_and_rotate(
+                        chunk, piece, token_operand, wq_operand, 1.0, out_0, adder_of(chunk, piece)
+                    )
+                    if first_chunk and piece == 0:
+                        wk_grouped = regroup_weight(wk_rows)
+                    if first_chunk and piece == PIECES - 1:
+                        wk_operand = quantise(wk_grouped, keep, "wk")
+                    if not last_chunk and piece == PIECES - 1:
+                        next_grouped = regroup_tokens(token_rows[chunk + 1], False)
+                for piece in range(PIECES):
+                    project_and_rotate(
+                        chunk,
+                        piece,
+                        token_operand,
+                        wk_operand,
+                        K_FACTOR,
+                        out_1,
+                        adder_of(chunk, PIECES + piece),
+                    )
+                    if not last_chunk and piece == 0:
+                        next_operand = quantise(next_grouped, quantised, "token")
+                token_operand = next_operand

@@ -22,8 +22,10 @@ CHUNK = CHUNK_BLOCKS * P
 CHUNKS_PER_BATCH = SEQ // CHUNK
 CHUNKS = BATCH * CHUNKS_PER_BATCH
 PIECE_BLOCKS = 2
-PIECES = CHUNK_BLOCKS // PIECE_BLOCKS
-VECTOR_ADDITIONS = 1
+STEPS = CHUNKS * CHUNK_BLOCKS
+K_LAG = 3
+SUM_LAG = 2
+GPSIMD_HEADS = 2
 
 FLOPS = 2 * BATCH * SEQ * EMBED * 2 * EMBED
 
@@ -36,14 +38,20 @@ def tile_nucleusxmultiscaleretention_pa_t_kernel(
         tc.tile_pool(name="keep", bufs=1) as keep,
         tc.tile_pool(name="tokens", bufs=CHUNKS) as tokens,
         tc.tile_pool(name="regroup", bufs=2) as regroup,
-        tc.tile_pool(name="quantised", bufs=2) as quantised,
-        tc.tile_pool(name="results", bufs=6) as results,
-        tc.tile_pool(name="products", bufs=4) as products,
+        tc.tile_pool(name="quantised", bufs=3) as quantised,
+        tc.tile_pool(name="q_products", bufs=5) as q_products,
+        tc.tile_pool(name="k_copies", bufs=3) as k_copies,
+        tc.tile_pool(name="k_products", bufs=4) as k_products,
+        tc.tile_pool(name="k_results", bufs=4) as k_results,
         tc.psum_pool(name="flipped", bufs=2) as flipped,
-        tc.psum_pool(name="sums", bufs=3) as sums,
+        tc.psum_pool(name="q_sums", bufs=2) as q_sums,
+        tc.psum_pool(name="k_sums", bufs=2) as k_sums,
+        tc.psum_pool(name="k_turns", bufs=2) as k_turns,
     ):
         identity = keep.tile([P, P], F32)
         make_identity(nc, identity[:])
+        identity_bf16 = keep.tile([P, P], BF16)
+        nc.vector.tensor_copy(out=identity_bf16[:], in_=identity[:])
         pair_swap = keep.tile([P, P], F32)
         identity_pairs = identity[:].rearrange("p (j two) -> p j two", two=2)
         pair_swap_pairs = pair_swap[:].rearrange("p (j two) -> p j two", two=2)
@@ -69,53 +77,62 @@ def tile_nucleusxmultiscaleretention_pa_t_kernel(
             )
             return rows
 
-        def load_table(table, tag):
-            rows = keep.tile([P, CHUNKS_PER_BATCH, CHUNK_BLOCKS, HEAD_DIM], BF16, name=tag)
+        def load_table(table, rows):
             nc.sync.dma_start(
-                out=rows[:].rearrange("p c i d -> p c (i d)"),
+                out=rows.rearrange("p c i d -> p c (i d)"),
                 in_=table.rearrange("(c p i) d -> p c (i d)", p=P, i=CHUNK_BLOCKS),
             )
-            return rows
 
         wq_rows = load_weight(wq, "wq")
         token_rows = [load_tokens(0)]
-        cos_table = load_table(cos, "cos_table")
-        sin_signed = load_table(sin, "sin_signed")
+        tables = keep.tile([P, 2, CHUNKS_PER_BATCH, CHUNK_BLOCKS, HEAD_DIM], BF16)
+        flat_tables = keep.tile([P, 2, CHUNKS_PER_BATCH, CHUNK], BF16)
+        sin_rows = keep.tile([P, CHUNKS_PER_BATCH, CHUNK_BLOCKS, HEAD_DIM], BF16)
+        load_table(sin, sin_rows[:])
+        load_table(cos, tables[:, 0])
         wk_rows = load_weight(wk, "wk")
         for chunk in range(1, CHUNKS):
             token_rows.append(load_tokens(chunk))
 
-        def regroup_rows(rows, permutation, grouped_words, vector_helps):
+        def turn_sin(place):
+            given = sin_rows[:, place].rearrange("p i (j two) -> p (i j) two", two=2)
+            made = tables[:, 1, place].rearrange("p i (j two) -> p (i j) two", two=2)
+            for goes_to, comes_from, sign in ((1, 0, -1.0), (0, 1, 1.0)):
+                nc.gpsimd.tensor_scalar(
+                    out=made[:, :, goes_to : goes_to + 1],
+                    in0=given[:, :, comes_from : comes_from + 1],
+                    scalar1=sign,
+                    scalar2=0.0,
+                    op0=MULT,
+                    op1=ADD,
+                )
+
+        def flatten_table(table, place):
+            bank = flipped.tile([P, CHUNK], BF16, name="flipped_bank")
+            for i in range(CHUNK_BLOCKS):
+                nc.tensor.transpose(
+                    bank[:, i * P : (i + 1) * P], tables[:, table, place, i, :], identity_bf16[:]
+                )
+            nc.scalar.copy(out=flat_tables[:, table, place, :], in_=bank[:])
+
+        def regroup_bank(rows, grouped, first, copy):
             words = rows[:].bitcast(F32)
-            for first in range(0, rows.shape[1] // EMBED, BANK_BLOCKS):
-                bank = flipped.tile([P, BANK], F32)
-                for j in range(BANK_BLOCKS):
-                    for u in range(2):
-                        nc.tensor.transpose(
-                            bank[:, (2 * j + u) * P : (2 * j + u + 1) * P],
-                            words[:, (first + j) * WORDS + u : (first + j + 1) * WORDS : 2],
-                            permutation[:],
-                        )
-                dense = grouped_words[:, first : first + BANK_BLOCKS]
-                hopping = bank[:].rearrange("p (j u r) -> p j r u", j=BANK_BLOCKS, u=2)
-                if vector_helps and first % (2 * BANK_BLOCKS) > 0:
-                    nc.vector.tensor_copy(out=dense, in_=hopping)
-                else:
-                    nc.scalar.copy(out=dense, in_=hopping)
+            bank = flipped.tile([P, BANK], F32, name="flipped_bank")
+            for j in range(BANK_BLOCKS):
+                for u in range(2):
+                    nc.tensor.transpose(
+                        bank[:, (2 * j + u) * P : (2 * j + u + 1) * P],
+                        words[:, (first + j) * WORDS + u : (first + j + 1) * WORDS : 2],
+                        identity[:],
+                    )
+            grouped_words = grouped[:].bitcast(F32).rearrange("p (j r u) -> p j r u", r=P, u=2)
+            copy(
+                out=grouped_words[:, first : first + BANK_BLOCKS],
+                in_=bank[:].rearrange("p (j u r) -> p j r u", j=BANK_BLOCKS, u=2),
+            )
 
-        def as_words(grouped):
-            return grouped[:].bitcast(F32).rearrange("p (j r u) -> p j r u", r=P, u=2)
-
-        def regroup_weight(rows):
-            grouped_weight = regroup.tile([P, 2 * EMBED * PACK], BF16, align_bytes=64)
-            regroup_rows(rows, identity, as_words(grouped_weight)[:, 0:HEADS], True)
-            regroup_rows(rows, pair_swap, as_words(grouped_weight)[:, HEADS : 2 * HEADS], True)
-            return grouped_weight
-
-        def regroup_tokens(rows, vector_helps):
-            grouped_tokens = regroup.tile([P, CHUNK * PACK], BF16, align_bytes=64)
-            regroup_rows(rows, identity, as_words(grouped_tokens), vector_helps)
-            return grouped_tokens
+        def new_grouped():
+            return regroup.tile([P, CHUNK_BLOCKS * P * PACK], BF16, name="grouped", align_bytes=64)
 
         def quantise(grouped, pool, tag):
             columns = grouped.shape[1] // PACK
@@ -124,86 +141,148 @@ def tile_nucleusxmultiscaleretention_pa_t_kernel(
             nc.vector.quantize_mx(out=codes[:].bitcast(FP8X4), scales=scales[:], in_=grouped[:])
             return codes, scales
 
-        def project_and_rotate(chunk, piece, token_operand, weight_operand, factor, out, adder):
+        def multiply(bank, stationary, columns, moving):
+            nc.tensor.matmul_mx(
+                out=bank[:],
+                lhsT=stationary[0][:, columns].bitcast(FP8X4),
+                lhsT_scale=stationary[1][:, columns],
+                rhs=moving[0][:].bitcast(FP8X4),
+                rhs_scale=moving[1][:],
+                start=True,
+                stop=True,
+            )
+
+        def chunk_rows(out, chunk):
             b, place = divmod(chunk, CHUNKS_PER_BATCH)
-            token_codes, token_scales = token_operand
-            weight_codes, weight_scales = weight_operand
-            rotated = results.tile([P, HEADS, PIECE_BLOCKS, HEAD_DIM], F32)
-            turned = products.tile([P, HEADS, PIECE_BLOCKS, HEAD_DIM], F32)
-            for j in range(PIECE_BLOCKS):
-                i = piece * PIECE_BLOCKS + j
-                block = slice(i * P, (i + 1) * P)
-                straight = sums.tile([P, BANK], F32)
-                swapped = sums.tile([P, BANK], F32)
-                for version, bank in enumerate((straight, swapped)):
-                    features = slice(version * EMBED, (version + 1) * EMBED)
-                    nc.tensor.matmul_mx(
-                        out=bank[:],
-                        lhsT=token_codes[:, block].bitcast(FP8X4),
-                        lhsT_scale=token_scales[:, block],
-                        rhs=weight_codes[:, features].bitcast(FP8X4),
-                        rhs_scale=weight_scales[:, features],
-                        start=True,
-                        stop=True,
-                    )
-                for bank, table, product in (
-                    (straight, cos_table, rotated),
-                    (swapped, sin_signed, turned),
-                ):
-                    nc.vector.scalar_tensor_tensor(
-                        out=product[:, :, j, :],
-                        in0=bank[:].rearrange("p (h d) -> p h d", h=HEADS),
-                        scalar=factor,
-                        in1=table[:, place, i, :].unsqueeze(1).to_broadcast([P, HEADS, HEAD_DIM]),
-                        op0=MULT,
-                        op1=MULT,
-                    )
-            adder.tensor_tensor(out=rotated[:], in0=rotated[:], in1=turned[:], op=ADD)
-            out_rows = out[b, :, place * CHUNK : (place + 1) * CHUNK, :].rearrange(
+            return out[b, :, place * CHUNK : (place + 1) * CHUNK, :].rearrange(
                 "h (p i) d -> p h i d", i=CHUNK_BLOCKS
             )
-            blocks = slice(piece * PIECE_BLOCKS, (piece + 1) * PIECE_BLOCKS)
-            nc.sync.dma_start(
-                out=out_rows[:, :, blocks, :].rearrange("p h i d -> p h (i d)"),
-                in_=rotated[:].rearrange("p h i d -> p h (i d)"),
+
+        def q_multiply(chunk, i, token_operand, wq_operand):
+            bank = q_sums.tile([P, BANK], F32, name="q_bank")
+            multiply(bank, token_operand, slice(i * P, (i + 1) * P), wq_operand)
+            return bank
+
+        def q_rotate(chunk, i, bank, products):
+            both = [P, 2, HEADS, HEAD_DIM]
+            nc.vector.tensor_tensor(
+                out=products[:, :, :, i % PIECE_BLOCKS, :],
+                in0=bank[:].rearrange("p (h d) -> p h d", h=HEADS).unsqueeze(1).to_broadcast(both),
+                in1=tables[:, :, chunk % CHUNKS_PER_BATCH, i, :].unsqueeze(2).to_broadcast(both),
+                op=MULT,
             )
 
-        def negate_even_features(place):
-            even = sin_signed[:, place].rearrange("p i (j two) -> p (i j) two", two=2)[:, :, 0:1]
-            nc.scalar.mul(out=even, in_=even, mul=-1.0)
+        def q_finish(chunk, i, products, adder):
+            straight = products[:, 0].rearrange("p h i (j two) -> p (h i j) two", two=2)
+            turned = products[:, 1].rearrange("p h i (j two) -> p (h i j) two", two=2)
+            adder.tensor_tensor(out=straight, in0=straight, in1=turned[:, :, ::-1], op=ADD)
+            blocks = slice(i + 1 - PIECE_BLOCKS, i + 1)
+            nc.sync.dma_start(
+                out=chunk_rows(out_0, chunk)[:, :, blocks, :].rearrange("p h i d -> p h (i d)"),
+                in_=products[:, 0].rearrange("p h i d -> p h (i d)"),
+            )
 
-        def adder_of(chunk, step):
-            additions_left = (CHUNKS - chunk) * 2 * PIECES - step
-            return nc.vector if additions_left <= VECTOR_ADDITIONS else nc.gpsimd
+        def k_multiply(h, token_operand, wk_operand, on_gpsimd):
+            bank = k_sums.tile([P, BANK], F32, name="k_bank")
+            multiply(bank, wk_operand, slice(h * P, (h + 1) * P), token_operand)
+            copied = None
+            if on_gpsimd:
+                copied = k_copies.tile([P, CHUNK], F32, name="k_copied")
+                nc.scalar.mul(out=copied[:], in_=bank[:], mul=K_FACTOR)
+            return bank, copied
+
+        def k_rotate(chunk, bank, copied):
+            place = chunk % CHUNKS_PER_BATCH
+            products = k_products.tile([P, 2, CHUNK], F32, name="k_pair")
+            if copied is not None:
+                nc.gpsimd.tensor_tensor(
+                    out=products[:, 1], in0=copied[:], in1=flat_tables[:, 1, place, :], op=MULT
+                )
+            by_vector = 2 if copied is None else 1
+            nc.vector.scalar_tensor_tensor(
+                out=products[:, 0:by_vector],
+                in0=bank[:].unsqueeze(1).to_broadcast([P, by_vector, CHUNK]),
+                scalar=K_FACTOR,
+                in1=flat_tables[:, 0:by_vector, place, :],
+                op0=MULT,
+                op1=MULT,
+            )
+            return products
+
+        def k_finish(chunk, h, products):
+            bank = k_turns.tile([P, CHUNK_BLOCKS, HEAD_DIM], F32, name="k_turn")
+            for i in range(CHUNK_BLOCKS):
+                block = slice(i * P, (i + 1) * P)
+                for table, permutation in ((0, identity), (1, pair_swap)):
+                    nc.tensor.matmul(
+                        out=bank[:, i, :],
+                        lhsT=products[:, table, block],
+                        rhs=permutation[:],
+                        is_transpose=True,
+                        start=table == 0,
+                        stop=table == 1,
+                    )
+            result = k_results.tile([P, CHUNK_BLOCKS, HEAD_DIM], F32, name="k_result")
+            nc.scalar.copy(out=result[:], in_=bank[:])
+            nc.sync.dma_start(
+                out=chunk_rows(out_1, chunk)[:, h].rearrange("p i d -> p (i d)"),
+                in_=result[:].rearrange("p i d -> p (i d)"),
+            )
 
         with tc.manual_schedule():
-            wq_operand = quantise(regroup_weight(wq_rows), keep, "wq")
-            token_operand = quantise(regroup_tokens(token_rows[0], True), quantised, "token")
-            for chunk in range(CHUNKS):
-                first_chunk = chunk == 0
-                last_chunk = chunk == CHUNKS - 1
-                if chunk < CHUNKS_PER_BATCH:
-                    negate_even_features(chunk)
-                for piece in range(PIECES):
-                    project_and_rotate(
-                        chunk, piece, token_operand, wq_operand, 1.0, out_0, adder_of(chunk, piece)
+            copies = (nc.scalar.copy, nc.vector.tensor_copy)
+            for place in range(CHUNKS_PER_BATCH):
+                turn_sin(place)
+            wq_grouped, grouped = new_grouped(), new_grouped()
+            for half in range(2):
+                regroup_bank(wq_rows, wq_grouped, half * BANK_BLOCKS, copies[half])
+            wq_operand = quantise(wq_grouped, keep, "wq")
+            for half in range(2):
+                regroup_bank(token_rows[0], grouped, half * BANK_BLOCKS, nc.scalar.copy)
+            token_operands = [quantise(grouped, quantised, "token")]
+            q_banks, k_banks, pairs = {}, {}, {}
+            q_banks[0] = q_multiply(0, 0, token_operands[0], wq_operand)
+            for step in range(STEPS + K_LAG + SUM_LAG):
+                chunk, i = divmod(step, CHUNK_BLOCKS)
+                k_step = step - K_LAG
+                sum_step = k_step - SUM_LAG
+                if 0 <= k_step + 1 < STEPS:
+                    k_chunk, h = divmod(k_step + 1, CHUNK_BLOCKS)
+                    k_banks[k_step + 1] = k_multiply(
+                        h, token_operands[k_chunk], wk_operand, h < GPSIMD_HEADS
                     )
-                    if first_chunk and piece == 0:
-                        wk_grouped = regroup_weight(wk_rows)
-                    if first_chunk and piece == PIECES - 1:
-                        wk_operand = quantise(wk_grouped, keep, "wk")
-                    if not last_chunk and piece == PIECES - 1:
-                        next_grouped = regroup_tokens(token_rows[chunk + 1], False)
-                for piece in range(PIECES):
-                    project_and_rotate(
-                        chunk,
-                        piece,
-                        token_operand,
-                        wk_operand,
-                        K_FACTOR,
-                        out_1,
-                        adder_of(chunk, PIECES + piece),
+                if step + 1 < STEPS:
+                    q_chunk, q_block = divmod(step + 1, CHUNK_BLOCKS)
+                    q_banks[step + 1] = q_multiply(
+                        q_chunk, q_block, token_operands[q_chunk], wq_operand
                     )
-                    if not last_chunk and piece == 0:
-                        next_operand = quantise(next_grouped, quantised, "token")
-                token_operand = next_operand
+                if 0 <= k_step < STEPS:
+                    pairs[k_step] = k_rotate(k_step // CHUNK_BLOCKS, *k_banks[k_step])
+                if step < STEPS:
+                    if i % PIECE_BLOCKS == 0:
+                        products = q_products.tile(
+                            [P, 2, HEADS, PIECE_BLOCKS, HEAD_DIM], F32, name="q_pair"
+                        )
+                    q_rotate(chunk, i, q_banks[step], products)
+                    if i % PIECE_BLOCKS == PIECE_BLOCKS - 1:
+                        q_finish(chunk, i, products, nc.gpsimd)
+                if step == 0:
+                    wk_grouped = keep.tile(
+                        [P, CHUNK_BLOCKS * P * PACK], BF16, name="wk_grouped", align_bytes=64
+                    )
+                    for half in range(2):
+                        regroup_bank(wk_rows, wk_grouped, half * BANK_BLOCKS, nc.scalar.copy)
+                if step == 1:
+                    wk_operand = quantise(wk_grouped, keep, "wk")
+                if chunk < CHUNKS_PER_BATCH and i < 2:
+                    flatten_table(i, chunk)
+                if chunk < CHUNKS - 1:
+                    if i == 0:
+                        grouped = new_grouped()
+                    if i < 2:
+                        regroup_bank(token_rows[chunk + 1], grouped, i * BANK_BLOCKS, nc.scalar.copy)
+                    if i == 2:
+                        token_operands.append(quantise(grouped, quantised, "token"))
+                if 0 <= sum_step < STEPS:
+                    sum_chunk, sum_head = divmod(sum_step, CHUNK_BLOCKS)
+                    k_finish(sum_chunk, sum_head, pairs[sum_step])

@@ -23,7 +23,7 @@ CHUNKS_PER_BATCH = SEQ // CHUNK
 CHUNKS = BATCH * CHUNKS_PER_BATCH
 PIECE_BLOCKS = 2
 STEPS = CHUNKS * CHUNK_BLOCKS
-K_LAG = 3
+K_START = 3
 SUM_LAG = 2
 GPSIMD_HEADS = 2
 
@@ -39,10 +39,10 @@ def tile_nucleusxmultiscaleretention_pa_t_kernel(
         tc.tile_pool(name="tokens", bufs=CHUNKS) as tokens,
         tc.tile_pool(name="regroup", bufs=2) as regroup,
         tc.tile_pool(name="quantised", bufs=3) as quantised,
-        tc.tile_pool(name="q_products", bufs=5) as q_products,
+        tc.tile_pool(name="q_products", bufs=7) as q_products,
         tc.tile_pool(name="k_copies", bufs=3) as k_copies,
-        tc.tile_pool(name="k_products", bufs=4) as k_products,
-        tc.tile_pool(name="k_results", bufs=4) as k_results,
+        tc.tile_pool(name="k_products", bufs=6) as k_products,
+        tc.tile_pool(name="k_results", bufs=8) as k_results,
         tc.psum_pool(name="flipped", bufs=2) as flipped,
         tc.psum_pool(name="q_sums", bufs=2) as q_sums,
         tc.psum_pool(name="k_sums", bufs=2) as k_sums,
@@ -58,41 +58,51 @@ def tile_nucleusxmultiscaleretention_pa_t_kernel(
         nc.vector.tensor_copy(out=pair_swap_pairs[:, :, 0:1], in_=identity_pairs[:, :, 1:2])
         nc.vector.tensor_copy(out=pair_swap_pairs[:, :, 1:2], in_=identity_pairs[:, :, 0:1])
 
-        def load_weight(w, tag):
-            rows = keep.tile([P, HEADS * EMBED], BF16, name=tag + "_rows")
+        def load_weight(w, rows, heads):
             nc.sync.dma_start(
-                out=rows[:].rearrange("p (h k) -> p h k", h=HEADS),
-                in_=w.rearrange("(h p) k -> p h k", p=P),
+                out=rows[:].rearrange("p (h k) -> p h k", h=HEADS)[:, heads],
+                in_=w.rearrange("(h p) k -> p h k", p=P)[:, heads],
             )
-            return rows
 
-        def load_tokens(chunk):
+        def load_tokens(chunk, rows, blocks):
             b, place = divmod(chunk, CHUNKS_PER_BATCH)
-            rows = tokens.tile([P, CHUNK_BLOCKS * EMBED], BF16, name="token_rows")
             nc.sync.dma_start(
-                out=rows[:],
+                out=rows[:].rearrange("p (i k) -> p i k", i=CHUNK_BLOCKS)[:, blocks],
                 in_=hidden_states[b, place * CHUNK : (place + 1) * CHUNK, :].rearrange(
-                    "(p i) k -> p (i k)", i=CHUNK_BLOCKS
-                ),
+                    "(p i) k -> p i k", i=CHUNK_BLOCKS
+                )[:, blocks],
             )
-            return rows
 
-        def load_table(table, rows):
+        def load_table(table, rows, places):
             nc.sync.dma_start(
-                out=rows.rearrange("p c i d -> p c (i d)"),
-                in_=table.rearrange("(c p i) d -> p c (i d)", p=P, i=CHUNK_BLOCKS),
+                out=rows.rearrange("p c i d -> p c (i d)")[:, places],
+                in_=table.rearrange("(c p i) d -> p c (i d)", p=P, i=CHUNK_BLOCKS)[:, places],
             )
 
-        wq_rows = load_weight(wq, "wq")
-        token_rows = [load_tokens(0)]
         tables = keep.tile([P, 2, CHUNKS_PER_BATCH, CHUNK_BLOCKS, HEAD_DIM], BF16)
         flat_tables = keep.tile([P, 2, CHUNKS_PER_BATCH, CHUNK], BF16)
         sin_rows = keep.tile([P, CHUNKS_PER_BATCH, CHUNK_BLOCKS, HEAD_DIM], BF16)
-        load_table(sin, sin_rows[:])
-        load_table(cos, tables[:, 0])
-        wk_rows = load_weight(wk, "wk")
-        for chunk in range(1, CHUNKS):
-            token_rows.append(load_tokens(chunk))
+        wq_rows = keep.tile([P, HEADS * EMBED], BF16)
+        wk_rows = keep.tile([P, HEADS * EMBED], BF16)
+        token_rows = []
+        for chunk in range(CHUNKS):
+            rows = tokens.tile([P, CHUNK_BLOCKS * EMBED], BF16, name="token_rows")
+            token_rows.append(rows)
+        halves = (slice(0, BANK_BLOCKS), slice(BANK_BLOCKS, 2 * BANK_BLOCKS))
+        first_place, later_places = slice(0, 1), slice(1, CHUNKS_PER_BATCH)
+        everything = slice(0, CHUNK_BLOCKS)
+        for half in halves:
+            load_weight(wq, wq_rows, half)
+        load_tokens(0, token_rows[0], halves[0])
+        load_table(sin, sin_rows[:], first_place)
+        load_table(cos, tables[:, 0], first_place)
+        load_tokens(0, token_rows[0], halves[1])
+        load_weight(wk, wk_rows, everything)
+        load_tokens(1, token_rows[1], everything)
+        load_table(sin, sin_rows[:], later_places)
+        load_table(cos, tables[:, 0], later_places)
+        for chunk in range(2, CHUNKS):
+            load_tokens(chunk, token_rows[chunk], everything)
 
         def turn_sin(place):
             given = sin_rows[:, place].rearrange("p i (j two) -> p (i j) two", two=2)
@@ -115,9 +125,8 @@ def tile_nucleusxmultiscaleretention_pa_t_kernel(
                 )
             nc.scalar.copy(out=flat_tables[:, table, place, :], in_=bank[:])
 
-        def regroup_bank(rows, grouped, first, copy):
+        def regroup_bank(rows, grouped, first, copy, bank):
             words = rows[:].bitcast(F32)
-            bank = flipped.tile([P, BANK], F32, name="flipped_bank")
             for j in range(BANK_BLOCKS):
                 for u in range(2):
                     nc.tensor.transpose(
@@ -131,15 +140,26 @@ def tile_nucleusxmultiscaleretention_pa_t_kernel(
                 in_=bank[:].rearrange("p (j u r) -> p j r u", j=BANK_BLOCKS, u=2),
             )
 
+        def new_bank():
+            return flipped.tile([P, BANK], F32, name="flipped_bank")
+
+        def new_k_turn():
+            return k_turns.tile([P, BANK], F32, name="k_turn")
+
         def new_grouped():
             return regroup.tile([P, CHUNK_BLOCKS * P * PACK], BF16, name="grouped", align_bytes=64)
 
-        def quantise(grouped, pool, tag):
-            columns = grouped.shape[1] // PACK
-            codes = pool.tile([P, columns], U32, name=tag + "_codes", align_bytes=64)
-            scales = pool.tile([P, columns], U8, name=tag + "_scales", align_bytes=64)
-            nc.vector.quantize_mx(out=codes[:].bitcast(FP8X4), scales=scales[:], in_=grouped[:])
+        def new_operand(pool, tag):
+            codes = pool.tile([P, CHUNK], U32, name=tag + "_codes", align_bytes=64)
+            scales = pool.tile([P, CHUNK], U8, name=tag + "_scales", align_bytes=64)
             return codes, scales
+
+        def quantise(grouped, operand, columns):
+            nc.vector.quantize_mx(
+                out=operand[0][:, columns].bitcast(FP8X4),
+                scales=operand[1][:, columns],
+                in_=grouped[:, columns.start * PACK : columns.stop * PACK],
+            )
 
         def multiply(bank, stationary, columns, moving):
             nc.tensor.matmul_mx(
@@ -172,14 +192,18 @@ def tile_nucleusxmultiscaleretention_pa_t_kernel(
                 op=MULT,
             )
 
-        def q_finish(chunk, i, products, adder):
-            straight = products[:, 0].rearrange("p h i (j two) -> p (h i j) two", two=2)
-            turned = products[:, 1].rearrange("p h i (j two) -> p (h i j) two", two=2)
-            adder.tensor_tensor(out=straight, in0=straight, in1=turned[:, :, ::-1], op=ADD)
-            blocks = slice(i + 1 - PIECE_BLOCKS, i + 1)
+        def q_add(chunk, blocks, products, adder):
+            first = blocks.start // PIECE_BLOCKS * PIECE_BLOCKS
+            part = products[:, :, :, blocks.start - first : blocks.stop - first]
+            straight = part[:, 0].rearrange("p h i (j two) -> p h (i j) two", two=2)
+            turned = part[:, 1].rearrange("p h i (j two) -> p h (i j) two", two=2)
+            adder.tensor_tensor(out=straight, in0=straight, in1=turned[:, :, :, ::-1], op=ADD)
+            return chunk, blocks, part
+
+        def q_store(chunk, blocks, part):
             nc.sync.dma_start(
                 out=chunk_rows(out_0, chunk)[:, :, blocks, :].rearrange("p h i d -> p h (i d)"),
-                in_=products[:, 0].rearrange("p h i d -> p h (i d)"),
+                in_=part[:, 0].rearrange("p h i d -> p h (i d)"),
             )
 
         def k_multiply(h, token_operand, wk_operand, on_gpsimd):
@@ -210,79 +234,92 @@ def tile_nucleusxmultiscaleretention_pa_t_kernel(
             return products
 
         def k_finish(chunk, h, products):
-            bank = k_turns.tile([P, CHUNK_BLOCKS, HEAD_DIM], F32, name="k_turn")
+            bank = new_k_turn()
             for i in range(CHUNK_BLOCKS):
                 block = slice(i * P, (i + 1) * P)
                 for table, permutation in ((0, identity), (1, pair_swap)):
                     nc.tensor.matmul(
-                        out=bank[:, i, :],
+                        out=bank[:, i * HEAD_DIM : (i + 1) * HEAD_DIM],
                         lhsT=products[:, table, block],
                         rhs=permutation[:],
                         is_transpose=True,
                         start=table == 0,
                         stop=table == 1,
                     )
-            result = k_results.tile([P, CHUNK_BLOCKS, HEAD_DIM], F32, name="k_result")
+            result = k_results.tile([P, CHUNK_BLOCKS * HEAD_DIM], F32, name="k_result")
             nc.scalar.copy(out=result[:], in_=bank[:])
             nc.sync.dma_start(
                 out=chunk_rows(out_1, chunk)[:, h].rearrange("p i d -> p (i d)"),
-                in_=result[:].rearrange("p i d -> p (i d)"),
+                in_=result[:],
             )
 
+        def heads_until(step):
+            return max(0, -((K_START - step) * STEPS // (STEPS - K_START)))
+
+        def heads_of(step):
+            return range(heads_until(step), min(STEPS, heads_until(step + 1)))
+
         with tc.manual_schedule():
-            copies = (nc.scalar.copy, nc.vector.tensor_copy)
-            for place in range(CHUNKS_PER_BATCH):
-                turn_sin(place)
+            turn_sin(0)
             wq_grouped, grouped = new_grouped(), new_grouped()
+            wk_grouped = keep.tile([P, CHUNK * PACK], BF16, align_bytes=64)
+            wq_operand, wk_operand = new_operand(keep, "wq"), new_operand(keep, "wk")
+            whole = slice(0, CHUNK)
+            operands = [new_operand(quantised, "token")]
+            regroup_bank(wq_rows, wq_grouped, 0, nc.scalar.copy, new_k_turn())
+            regroup_bank(wq_rows, wq_grouped, BANK_BLOCKS, nc.vector.tensor_copy, new_k_turn())
             for half in range(2):
-                regroup_bank(wq_rows, wq_grouped, half * BANK_BLOCKS, copies[half])
-            wq_operand = quantise(wq_grouped, keep, "wq")
-            for half in range(2):
-                regroup_bank(token_rows[0], grouped, half * BANK_BLOCKS, nc.scalar.copy)
-            token_operands = [quantise(grouped, quantised, "token")]
-            q_banks, k_banks, pairs = {}, {}, {}
-            q_banks[0] = q_multiply(0, 0, token_operands[0], wq_operand)
-            for step in range(STEPS + K_LAG + SUM_LAG):
+                regroup_bank(token_rows[0], grouped, half * BANK_BLOCKS, nc.scalar.copy, new_bank())
+            quantise(wq_grouped, wq_operand, whole)
+            quantise(grouped, operands[0], slice(0, CHUNK // 2))
+            q_banks, k_banks, pairs, q_results = {}, {}, {}, {}
+            q_banks[0] = q_multiply(0, 0, operands[0], wq_operand)
+            for step in range(STEPS + SUM_LAG):
                 chunk, i = divmod(step, CHUNK_BLOCKS)
-                k_step = step - K_LAG
-                sum_step = k_step - SUM_LAG
-                if 0 <= k_step + 1 < STEPS:
-                    k_chunk, h = divmod(k_step + 1, CHUNK_BLOCKS)
-                    k_banks[k_step + 1] = k_multiply(
-                        h, token_operands[k_chunk], wk_operand, h < GPSIMD_HEADS
-                    )
+                for k_step in heads_of(step):
+                    pairs[k_step] = k_rotate(k_step // CHUNK_BLOCKS, *k_banks[k_step])
+                for k_step in heads_of(step + 1):
+                    k_chunk, h = divmod(k_step, CHUNK_BLOCKS)
+                    k_banks[k_step] = k_multiply(h, operands[k_chunk], wk_operand, h < GPSIMD_HEADS)
                 if step + 1 < STEPS:
                     q_chunk, q_block = divmod(step + 1, CHUNK_BLOCKS)
-                    q_banks[step + 1] = q_multiply(
-                        q_chunk, q_block, token_operands[q_chunk], wq_operand
-                    )
-                if 0 <= k_step < STEPS:
-                    pairs[k_step] = k_rotate(k_step // CHUNK_BLOCKS, *k_banks[k_step])
+                    q_banks[step + 1] = q_multiply(q_chunk, q_block, operands[q_chunk], wq_operand)
                 if step < STEPS:
                     if i % PIECE_BLOCKS == 0:
                         products = q_products.tile(
                             [P, 2, HEADS, PIECE_BLOCKS, HEAD_DIM], F32, name="q_pair"
                         )
                     q_rotate(chunk, i, q_banks[step], products)
-                    if i % PIECE_BLOCKS == PIECE_BLOCKS - 1:
-                        q_finish(chunk, i, products, nc.gpsimd)
+                    if step >= STEPS - PIECE_BLOCKS:
+                        adder = nc.vector if step == STEPS - 1 else nc.gpsimd
+                        q_results[step] = q_add(chunk, slice(i, i + 1), products, adder)
+                    elif i % PIECE_BLOCKS == PIECE_BLOCKS - 1:
+                        blocks = slice(i + 1 - PIECE_BLOCKS, i + 1)
+                        q_results[step] = q_add(chunk, blocks, products, nc.gpsimd)
                 if step == 0:
-                    wk_grouped = keep.tile(
-                        [P, CHUNK_BLOCKS * P * PACK], BF16, name="wk_grouped", align_bytes=64
-                    )
+                    quantise(grouped, operands[0], slice(CHUNK // 2, CHUNK))
                     for half in range(2):
-                        regroup_bank(wk_rows, wk_grouped, half * BANK_BLOCKS, nc.scalar.copy)
+                        regroup_bank(wk_rows, wk_grouped, half * BANK_BLOCKS, nc.scalar.copy, new_bank())
                 if step == 1:
-                    wk_operand = quantise(wk_grouped, keep, "wk")
-                if chunk < CHUNKS_PER_BATCH and i < 2:
-                    flatten_table(i, chunk)
+                    quantise(wk_grouped, wk_operand, whole)
+                if chunk == 0 and i < 2:
+                    flatten_table(i, 0)
+                if chunk < CHUNKS_PER_BATCH - 1:
+                    if i == 0:
+                        turn_sin(chunk + 1)
+                    if i >= 2:
+                        flatten_table(i - 2, chunk + 1)
                 if chunk < CHUNKS - 1:
                     if i == 0:
                         grouped = new_grouped()
+                        operands.append(new_operand(quantised, "token"))
                     if i < 2:
-                        regroup_bank(token_rows[chunk + 1], grouped, i * BANK_BLOCKS, nc.scalar.copy)
+                        regroup_bank(
+                            token_rows[chunk + 1], grouped, i * BANK_BLOCKS, nc.scalar.copy, new_bank()
+                        )
                     if i == 2:
-                        token_operands.append(quantise(grouped, quantised, "token"))
-                if 0 <= sum_step < STEPS:
-                    sum_chunk, sum_head = divmod(sum_step, CHUNK_BLOCKS)
-                    k_finish(sum_chunk, sum_head, pairs[sum_step])
+                        quantise(grouped, operands[chunk + 1], whole)
+                for k_step in heads_of(step - SUM_LAG):
+                    k_finish(*divmod(k_step, CHUNK_BLOCKS), pairs[k_step])
+                if step - 1 in q_results:
+                    q_store(*q_results[step - 1])

@@ -23,9 +23,9 @@ CHUNKS_PER_BATCH = SEQ // CHUNK
 CHUNKS = BATCH * CHUNKS_PER_BATCH
 PIECE_BLOCKS = 2
 STEPS = CHUNKS * CHUNK_BLOCKS
-K_START = 3
+K_START = 2
 SUM_LAG = 2
-GPSIMD_HEADS = 2
+GPSIMD_STEPS = (1, 2)
 
 FLOPS = 2 * BATCH * SEQ * EMBED * 2 * EMBED
 
@@ -37,11 +37,11 @@ def tile_nucleusxmultiscaleretention_pa_t_kernel(
     with (
         tc.tile_pool(name="keep", bufs=1) as keep,
         tc.tile_pool(name="tokens", bufs=CHUNKS) as tokens,
-        tc.tile_pool(name="regroup", bufs=2) as regroup,
+        tc.tile_pool(name="regroup", bufs=3) as regroup,
         tc.tile_pool(name="quantised", bufs=3) as quantised,
         tc.tile_pool(name="q_products", bufs=7) as q_products,
         tc.tile_pool(name="k_copies", bufs=3) as k_copies,
-        tc.tile_pool(name="k_products", bufs=6) as k_products,
+        tc.tile_pool(name="k_products", bufs=8) as k_products,
         tc.tile_pool(name="k_results", bufs=8) as k_results,
         tc.psum_pool(name="flipped", bufs=2) as flipped,
         tc.psum_pool(name="q_sums", bufs=2) as q_sums,
@@ -98,8 +98,8 @@ def tile_nucleusxmultiscaleretention_pa_t_kernel(
         load_table(cos, tables[:, 0], first_place)
         load_tokens(0, token_rows[0], halves[1])
         load_weight(wk, wk_rows, everything)
-        load_tokens(1, token_rows[1], everything)
         load_table(sin, sin_rows[:], later_places)
+        load_tokens(1, token_rows[1], everything)
         load_table(cos, tables[:, 0], later_places)
         for chunk in range(2, CHUNKS):
             load_tokens(chunk, token_rows[chunk], everything)
@@ -178,7 +178,7 @@ def tile_nucleusxmultiscaleretention_pa_t_kernel(
                 "h (p i) d -> p h i d", i=CHUNK_BLOCKS
             )
 
-        def q_multiply(chunk, i, token_operand, wq_operand):
+        def q_multiply(i, token_operand, wq_operand):
             bank = q_sums.tile([P, BANK], F32, name="q_bank")
             multiply(bank, token_operand, slice(i * P, (i + 1) * P), wq_operand)
             return bank
@@ -192,46 +192,44 @@ def tile_nucleusxmultiscaleretention_pa_t_kernel(
                 op=MULT,
             )
 
-        def q_add(chunk, blocks, products, adder):
-            first = blocks.start // PIECE_BLOCKS * PIECE_BLOCKS
-            part = products[:, :, :, blocks.start - first : blocks.stop - first]
-            straight = part[:, 0].rearrange("p h i (j two) -> p h (i j) two", two=2)
-            turned = part[:, 1].rearrange("p h i (j two) -> p h (i j) two", two=2)
+        def q_add(i, products, adder):
+            part = products[:, :, :, i % PIECE_BLOCKS]
+            straight = part[:, 0].rearrange("p h (j two) -> p h j two", two=2)
+            turned = part[:, 1].rearrange("p h (j two) -> p h j two", two=2)
             adder.tensor_tensor(out=straight, in0=straight, in1=turned[:, :, :, ::-1], op=ADD)
-            return chunk, blocks, part
 
-        def q_store(chunk, blocks, part):
+        def q_store(chunk, blocks, products):
+            first = blocks.start % PIECE_BLOCKS
+            part = products[:, 0, :, first : first + blocks.stop - blocks.start]
             nc.sync.dma_start(
                 out=chunk_rows(out_0, chunk)[:, :, blocks, :].rearrange("p h i d -> p h (i d)"),
-                in_=part[:, 0].rearrange("p h i d -> p h (i d)"),
+                in_=part.rearrange("p h i d -> p h (i d)"),
             )
 
-        def k_multiply(h, token_operand, wk_operand, on_gpsimd):
+        def k_multiply(chunk, h, token_operand, wk_operand, gpsimd_helps):
             bank = k_sums.tile([P, BANK], F32, name="k_bank")
             multiply(bank, wk_operand, slice(h * P, (h + 1) * P), token_operand)
-            copied = None
-            if on_gpsimd:
+            products = k_products.tile([P, 2, CHUNK], F32, name="k_pair")
+            if gpsimd_helps:
                 copied = k_copies.tile([P, CHUNK], F32, name="k_copied")
                 nc.scalar.mul(out=copied[:], in_=bank[:], mul=K_FACTOR)
-            return bank, copied
-
-        def k_rotate(chunk, bank, copied):
-            place = chunk % CHUNKS_PER_BATCH
-            products = k_products.tile([P, 2, CHUNK], F32, name="k_pair")
-            if copied is not None:
                 nc.gpsimd.tensor_tensor(
-                    out=products[:, 1], in0=copied[:], in1=flat_tables[:, 1, place, :], op=MULT
+                    out=products[:, 1],
+                    in0=copied[:],
+                    in1=flat_tables[:, 1, chunk % CHUNKS_PER_BATCH, :],
+                    op=MULT,
                 )
-            by_vector = 2 if copied is None else 1
+            return bank, products, 1 if gpsimd_helps else 2
+
+        def k_rotate(chunk, bank, products, by_vector):
             nc.vector.scalar_tensor_tensor(
                 out=products[:, 0:by_vector],
                 in0=bank[:].unsqueeze(1).to_broadcast([P, by_vector, CHUNK]),
                 scalar=K_FACTOR,
-                in1=flat_tables[:, 0:by_vector, place, :],
+                in1=flat_tables[:, 0:by_vector, chunk % CHUNKS_PER_BATCH, :],
                 op0=MULT,
                 op1=MULT,
             )
-            return products
 
         def k_finish(chunk, h, products):
             bank = new_k_turn()
@@ -254,14 +252,17 @@ def tile_nucleusxmultiscaleretention_pa_t_kernel(
             )
 
         def heads_until(step):
-            return max(0, -((K_START - step) * STEPS // (STEPS - K_START)))
+            if step >= STEPS:
+                return STEPS
+            return max(0, (step - K_START) * (STEPS - 2) // (STEPS - 1 - K_START))
 
         def heads_of(step):
-            return range(heads_until(step), min(STEPS, heads_until(step + 1)))
+            return range(heads_until(step), heads_until(step + 1))
 
         with tc.manual_schedule():
-            turn_sin(0)
-            wq_grouped, grouped = new_grouped(), new_grouped()
+            for place in range(CHUNKS_PER_BATCH):
+                turn_sin(place)
+            wq_grouped, grouped_first = new_grouped(), new_grouped()
             wk_grouped = keep.tile([P, CHUNK * PACK], BF16, align_bytes=64)
             wq_operand, wk_operand = new_operand(keep, "wq"), new_operand(keep, "wk")
             whole = slice(0, CHUNK)
@@ -269,57 +270,79 @@ def tile_nucleusxmultiscaleretention_pa_t_kernel(
             regroup_bank(wq_rows, wq_grouped, 0, nc.scalar.copy, new_k_turn())
             regroup_bank(wq_rows, wq_grouped, BANK_BLOCKS, nc.vector.tensor_copy, new_k_turn())
             for half in range(2):
-                regroup_bank(token_rows[0], grouped, half * BANK_BLOCKS, nc.scalar.copy, new_bank())
+                regroup_bank(token_rows[0], grouped_first, half * BANK_BLOCKS, nc.scalar.copy, new_bank())
             quantise(wq_grouped, wq_operand, whole)
-            quantise(grouped, operands[0], slice(0, CHUNK // 2))
-            q_banks, k_banks, pairs, q_results = {}, {}, {}, {}
-            q_banks[0] = q_multiply(0, 0, operands[0], wq_operand)
+            quantise(grouped_first, operands[0], slice(0, CHUNK // 2))
+            q_banks, k_banks, q_results = {}, {}, {}
+            q_banks[0] = q_multiply(0, operands[0], wq_operand)
+            for table in range(2):
+                flatten_table(table, 0)
+            def regroup_tokens(chunk):
+                grouped = new_grouped()
+                for half in range(2):
+                    regroup_bank(
+                        token_rows[chunk], grouped, half * BANK_BLOCKS, nc.scalar.copy, new_bank()
+                    )
+                return grouped
+
+            def fill_k_banks(k_steps, step):
+                for k_step in k_steps:
+                    chunk, h = divmod(k_step, CHUNK_BLOCKS)
+                    gpsimd_helps = step % CHUNK_BLOCKS in GPSIMD_STEPS and k_step == heads_of(step)[0]
+                    k_banks[k_step] = k_multiply(chunk, h, operands[chunk], wk_operand, gpsimd_helps)
+
+            def store_q(step):
+                chunk, i = divmod(step, CHUNK_BLOCKS)
+                last = step >= STEPS - PIECE_BLOCKS
+                if last:
+                    q_store(chunk, slice(i, i + 1), q_results[step])
+                elif i % PIECE_BLOCKS == PIECE_BLOCKS - 1:
+                    q_store(chunk, slice(i + 1 - PIECE_BLOCKS, i + 1), q_results[step])
+
             for step in range(STEPS + SUM_LAG):
                 chunk, i = divmod(step, CHUNK_BLOCKS)
-                for k_step in heads_of(step):
-                    pairs[k_step] = k_rotate(k_step // CHUNK_BLOCKS, *k_banks[k_step])
-                for k_step in heads_of(step + 1):
-                    k_chunk, h = divmod(k_step, CHUNK_BLOCKS)
-                    k_banks[k_step] = k_multiply(h, operands[k_chunk], wk_operand, h < GPSIMD_HEADS)
-                if step + 1 < STEPS:
-                    q_chunk, q_block = divmod(step + 1, CHUNK_BLOCKS)
-                    q_banks[step + 1] = q_multiply(q_chunk, q_block, operands[q_chunk], wq_operand)
+                first_step, last_step = i == 0, i == CHUNK_BLOCKS - 1
+                next_heads = heads_of(step + 1)
+                if step > 1:
+                    fill_k_banks(next_heads[:1], step + 1)
+                if step != K_START:
+                    for k_step in heads_of(step):
+                        k_rotate(k_step // CHUNK_BLOCKS, *k_banks[k_step])
                 if step < STEPS:
                     if i % PIECE_BLOCKS == 0:
                         products = q_products.tile(
                             [P, 2, HEADS, PIECE_BLOCKS, HEAD_DIM], F32, name="q_pair"
                         )
                     q_rotate(chunk, i, q_banks[step], products)
-                    if step >= STEPS - PIECE_BLOCKS:
-                        adder = nc.vector if step == STEPS - 1 else nc.gpsimd
-                        q_results[step] = q_add(chunk, slice(i, i + 1), products, adder)
-                    elif i % PIECE_BLOCKS == PIECE_BLOCKS - 1:
-                        blocks = slice(i + 1 - PIECE_BLOCKS, i + 1)
-                        q_results[step] = q_add(chunk, blocks, products, nc.gpsimd)
+                    q_add(i, products, nc.vector if step == STEPS - 1 else nc.gpsimd)
+                    q_results[step] = products
+                if step == K_START:
+                    for k_step in heads_of(step):
+                        k_rotate(k_step // CHUNK_BLOCKS, *k_banks[k_step])
+                if last_step and chunk < CHUNKS - 1:
+                    operands.append(new_operand(quantised, "token"))
+                    quantise(prepared, operands[chunk + 1], whole)
                 if step == 0:
-                    quantise(grouped, operands[0], slice(CHUNK // 2, CHUNK))
-                    for half in range(2):
-                        regroup_bank(wk_rows, wk_grouped, half * BANK_BLOCKS, nc.scalar.copy, new_bank())
+                    quantise(grouped_first, operands[0], slice(CHUNK // 2, CHUNK))
+                if not last_step and step + 1 < STEPS:
+                    q_banks[step + 1] = q_multiply(i + 1, operands[chunk], wq_operand)
                 if step == 1:
                     quantise(wk_grouped, wk_operand, whole)
-                if chunk == 0 and i < 2:
-                    flatten_table(i, 0)
-                if chunk < CHUNKS_PER_BATCH - 1:
-                    if i == 0:
-                        turn_sin(chunk + 1)
-                    if i >= 2:
-                        flatten_table(i - 2, chunk + 1)
-                if chunk < CHUNKS - 1:
-                    if i == 0:
-                        grouped = new_grouped()
-                        operands.append(new_operand(quantised, "token"))
-                    if i < 2:
-                        regroup_bank(
-                            token_rows[chunk + 1], grouped, i * BANK_BLOCKS, nc.scalar.copy, new_bank()
-                        )
-                    if i == 2:
-                        quantise(grouped, operands[chunk + 1], whole)
+                    fill_k_banks(next_heads, step + 1)
+                else:
+                    fill_k_banks(next_heads[1:], step + 1)
                 for k_step in heads_of(step - SUM_LAG):
-                    k_finish(*divmod(k_step, CHUNK_BLOCKS), pairs[k_step])
-                if step - 1 in q_results:
-                    q_store(*q_results[step - 1])
+                    k_finish(*divmod(k_step, CHUNK_BLOCKS), k_banks[k_step][1])
+                if step == 0:
+                    for half in range(2):
+                        regroup_bank(wk_rows, wk_grouped, half * BANK_BLOCKS, nc.scalar.copy, new_bank())
+                if chunk < CHUNKS_PER_BATCH - 1 and i >= 2:
+                    flatten_table(i - 2, chunk + 1)
+                if step == 2:
+                    prepared = regroup_tokens(1)
+                if last_step and chunk < CHUNKS - 2:
+                    prepared = regroup_tokens(chunk + 2)
+                if last_step and step + 1 < STEPS:
+                    q_banks[step + 1] = q_multiply(0, operands[chunk + 1], wq_operand)
+                if 0 < step <= STEPS:
+                    store_q(step - 1)

@@ -16,12 +16,15 @@ K_FACTOR = HEAD_DIM**-0.5
 PACK = 4
 WORDS = EMBED // 2
 BANK = 512
+HALVES = 2
 BANK_BLOCKS = BANK // WORDS
 CHUNK_BLOCKS = 4
 CHUNK = CHUNK_BLOCKS * P
 CHUNKS_PER_BATCH = SEQ // CHUNK
 CHUNKS = BATCH * CHUNKS_PER_BATCH
 PIECE_BLOCKS = 2
+GROUPS = ((0,), (1,), (2, 3), (4, 5), (6, 7))
+GROUP = 2 * CHUNK
 STEPS = CHUNKS * CHUNK_BLOCKS
 K_START = 2
 SUM_LAG = 2
@@ -147,12 +150,15 @@ def tile_nucleusxmultiscaleretention_pa_t_kernel(
             return k_turns.tile([P, BANK], F32, name="k_turn")
 
         def new_grouped():
-            return regroup.tile([P, CHUNK_BLOCKS * P * PACK], BF16, name="grouped", align_bytes=64)
+            return regroup.tile([P, GROUP * PACK], BF16, name="grouped", align_bytes=64)
 
-        def new_operand(pool, tag):
-            codes = pool.tile([P, CHUNK], U32, name=tag + "_codes", align_bytes=64)
-            scales = pool.tile([P, CHUNK], U8, name=tag + "_scales", align_bytes=64)
+        def new_operand(pool, tag, columns):
+            codes = pool.tile([P, columns], U32, name=tag + "_codes", align_bytes=64)
+            scales = pool.tile([P, columns], U8, name=tag + "_scales", align_bytes=64)
             return codes, scales
+
+        def part_of(operand, columns):
+            return operand[0][:, columns], operand[1][:, columns]
 
         def quantise(grouped, operand, columns):
             nc.vector.quantize_mx(
@@ -178,9 +184,10 @@ def tile_nucleusxmultiscaleretention_pa_t_kernel(
                 "h (p i) d -> p h i d", i=CHUNK_BLOCKS
             )
 
-        def q_multiply(i, token_operand, wq_operand):
+        def q_multiply(step, operands, wq_operand):
+            chunk, i = divmod(step, CHUNK_BLOCKS)
             bank = q_sums.tile([P, BANK], F32, name="q_bank")
-            multiply(bank, token_operand, slice(i * P, (i + 1) * P), wq_operand)
+            multiply(bank, operands[chunk], slice(i * P, (i + 1) * P), wq_operand)
             return bank
 
         def q_rotate(chunk, i, bank, products):
@@ -192,10 +199,9 @@ def tile_nucleusxmultiscaleretention_pa_t_kernel(
                 op=MULT,
             )
 
-        def q_add(i, products, adder):
-            part = products[:, :, :, i % PIECE_BLOCKS]
-            straight = part[:, 0].rearrange("p h (j two) -> p h j two", two=2)
-            turned = part[:, 1].rearrange("p h (j two) -> p h j two", two=2)
+        def q_add(blocks, products, adder):
+            straight = products[:, 0, :, blocks].rearrange("p h i (j two) -> p h (i j) two", two=2)
+            turned = products[:, 1, :, blocks].rearrange("p h i (j two) -> p h (i j) two", two=2)
             adder.tensor_tensor(out=straight, in0=straight, in1=turned[:, :, :, ::-1], op=ADD)
 
         def q_store(chunk, blocks, products):
@@ -262,11 +268,14 @@ def tile_nucleusxmultiscaleretention_pa_t_kernel(
         with tc.manual_schedule():
             for place in range(CHUNKS_PER_BATCH):
                 turn_sin(place)
-            wq_grouped, grouped_first = new_grouped(), new_grouped()
+            wq_grouped_tile, first_tile = new_grouped(), new_grouped()
             wk_grouped = keep.tile([P, CHUNK * PACK], BF16, align_bytes=64)
-            wq_operand, wk_operand = new_operand(keep, "wq"), new_operand(keep, "wk")
+            wq_operand, wk_operand = new_operand(keep, "wq", CHUNK), new_operand(keep, "wk", CHUNK)
             whole = slice(0, CHUNK)
-            operands = [new_operand(quantised, "token")]
+            first_operand = new_operand(quantised, "token", GROUP)
+            operands = [part_of(first_operand, whole)]
+            wq_grouped = wq_grouped_tile[:, 0 : CHUNK * PACK]
+            grouped_first = first_tile[:, 0 : CHUNK * PACK]
             regroup_bank(wq_rows, wq_grouped, 0, nc.scalar.copy, new_k_turn())
             regroup_bank(wq_rows, wq_grouped, BANK_BLOCKS, nc.vector.tensor_copy, new_k_turn())
             for half in range(2):
@@ -274,16 +283,18 @@ def tile_nucleusxmultiscaleretention_pa_t_kernel(
             quantise(wq_grouped, wq_operand, whole)
             quantise(grouped_first, operands[0], slice(0, CHUNK // 2))
             q_banks, k_banks, q_results = {}, {}, {}
-            q_banks[0] = q_multiply(0, operands[0], wq_operand)
+            gate = keep.tile([P, 1], U8)
+            q_banks[0] = q_multiply(0, operands, wq_operand)
             for table in range(2):
                 flatten_table(table, 0)
-            def regroup_tokens(chunk):
-                grouped = new_grouped()
-                for half in range(2):
-                    regroup_bank(
-                        token_rows[chunk], grouped, half * BANK_BLOCKS, nc.scalar.copy, new_bank()
-                    )
-                return grouped
+            bank_of, group_of = {}, {}
+            for group in range(1, len(GROUPS)):
+                quantise_step = GROUPS[group][0] * CHUNK_BLOCKS - 1
+                group_of[quantise_step] = group
+                banks = len(GROUPS[group]) * HALVES
+                for bank in range(banks):
+                    bank_of[quantise_step - banks + bank] = group, bank
+            grouped_tokens = {}
 
             def fill_k_banks(k_steps, step):
                 for k_step in k_steps:
@@ -301,7 +312,6 @@ def tile_nucleusxmultiscaleretention_pa_t_kernel(
 
             for step in range(STEPS + SUM_LAG):
                 chunk, i = divmod(step, CHUNK_BLOCKS)
-                first_step, last_step = i == 0, i == CHUNK_BLOCKS - 1
                 next_heads = heads_of(step + 1)
                 if step > 1:
                     fill_k_banks(next_heads[:1], step + 1)
@@ -314,18 +324,26 @@ def tile_nucleusxmultiscaleretention_pa_t_kernel(
                             [P, 2, HEADS, PIECE_BLOCKS, HEAD_DIM], F32, name="q_pair"
                         )
                     q_rotate(chunk, i, q_banks[step], products)
-                    q_add(i, products, nc.vector if step == STEPS - 1 else nc.gpsimd)
                     q_results[step] = products
                 if step == K_START:
                     for k_step in heads_of(step):
                         k_rotate(k_step // CHUNK_BLOCKS, *k_banks[k_step])
-                if last_step and chunk < CHUNKS - 1:
-                    operands.append(new_operand(quantised, "token"))
-                    quantise(prepared, operands[chunk + 1], whole)
+                if step in group_of:
+                    group = group_of[step]
+                    operand = new_operand(quantised, "token", GROUP)
+                    quantise(grouped_tokens[group], operand, slice(0, len(GROUPS[group]) * CHUNK))
+                    for place in range(len(GROUPS[group])):
+                        operands.append(part_of(operand, slice(place * CHUNK, (place + 1) * CHUNK)))
+                    nc.gpsimd.tensor_copy(out=gate[:], in_=operand[1][:, 0:1])
                 if step == 0:
                     quantise(grouped_first, operands[0], slice(CHUNK // 2, CHUNK))
-                if not last_step and step + 1 < STEPS:
-                    q_banks[step + 1] = q_multiply(i + 1, operands[chunk], wq_operand)
+                j = i % PIECE_BLOCKS
+                if STEPS - PIECE_BLOCKS <= step < STEPS:
+                    q_add(slice(j, j + 1), products, nc.vector if step == STEPS - 1 else nc.gpsimd)
+                elif step < STEPS and j == PIECE_BLOCKS - 1:
+                    q_add(slice(0, PIECE_BLOCKS), products, nc.gpsimd)
+                if step not in group_of and step + 1 < STEPS:
+                    q_banks[step + 1] = q_multiply(step + 1, operands, wq_operand)
                 if step == 1:
                     quantise(wk_grouped, wk_operand, whole)
                     fill_k_banks(next_heads, step + 1)
@@ -338,11 +356,20 @@ def tile_nucleusxmultiscaleretention_pa_t_kernel(
                         regroup_bank(wk_rows, wk_grouped, half * BANK_BLOCKS, nc.scalar.copy, new_bank())
                 if chunk < CHUNKS_PER_BATCH - 1 and i >= 2:
                     flatten_table(i - 2, chunk + 1)
-                if step == 2:
-                    prepared = regroup_tokens(1)
-                if last_step and chunk < CHUNKS - 2:
-                    prepared = regroup_tokens(chunk + 2)
-                if last_step and step + 1 < STEPS:
-                    q_banks[step + 1] = q_multiply(0, operands[chunk + 1], wq_operand)
+                if step in bank_of:
+                    group, bank = bank_of[step]
+                    if bank == 0:
+                        grouped_tokens[group] = new_grouped()
+                    place, half = divmod(bank, HALVES)
+                    columns = slice(place * CHUNK * PACK, (place + 1) * CHUNK * PACK)
+                    regroup_bank(
+                        token_rows[GROUPS[group][place]],
+                        grouped_tokens[group][:, columns],
+                        half * BANK_BLOCKS,
+                        nc.scalar.copy,
+                        new_bank(),
+                    )
+                if step in group_of:
+                    q_banks[step + 1] = q_multiply(step + 1, operands, wq_operand)
                 if 0 < step <= STEPS:
                     store_q(step - 1)

import concourse.mybir as mybir
from concourse.masks import make_identity

F32 = mybir.dt.float32
BF16 = mybir.dt.bfloat16
U32 = mybir.dt.uint32
U8 = mybir.dt.uint8
FP8X4 = mybir.dt.float8_e4m3fn_x4
MULT = mybir.AluOpType.mult
ADD = mybir.AluOpType.add

P = 128
BATCH, SEQ, EMBED, HEADS = 2, 2048, 512, 4
HEAD_DIM = EMBED // HEADS
K_FACTOR = HEAD_DIM**-0.5
PACK = 4
WORDS = EMBED // 2
BANK = 512
HALVES = 2
BANK_BLOCKS = BANK // WORDS
CHUNK_BLOCKS = 4
CHUNK = CHUNK_BLOCKS * P
CHUNKS_PER_BATCH = SEQ // CHUNK
CHUNKS = BATCH * CHUNKS_PER_BATCH
PIECE_BLOCKS = 2
GROUPS = ((0,), (1,), (2, 3), (4, 5), (6, 7))
GROUP = 2 * CHUNK
STEPS = CHUNKS * CHUNK_BLOCKS
K_START = 2
SUM_LAG = 2
GPSIMD_STEPS = (1, 2)

FLOPS = 2 * BATCH * SEQ * EMBED * 2 * EMBED


def tile_nucleusxmultiscaleretention_pa_t_kernel(
    tc, hidden_states, wq, wk, sin, cos, out_0, out_1
):
    nc = tc.nc
    with (
        tc.tile_pool(name="keep", bufs=1) as keep,
        tc.tile_pool(name="tokens", bufs=CHUNKS) as tokens,
        tc.tile_pool(name="regroup", bufs=3) as regroup,
        tc.tile_pool(name="quantised", bufs=3) as quantised,
        tc.tile_pool(name="q_products", bufs=7) as q_products,
        tc.tile_pool(name="k_copies", bufs=3) as k_copies,
        tc.tile_pool(name="k_products", bufs=8) as k_products,
        tc.tile_pool(name="k_results", bufs=8) as k_results,
        tc.psum_pool(name="flipped", bufs=2) as flipped,
        tc.psum_pool(name="q_sums", bufs=2) as q_sums,
        tc.psum_pool(name="k_sums", bufs=2) as k_sums,
        tc.psum_pool(name="k_turns", bufs=2) as k_turns,
    ):
        identity = keep.tile([P, P], F32)
        make_identity(nc, identity[:])
        identity_bf16 = keep.tile([P, P], BF16)
        nc.vector.tensor_copy(out=identity_bf16[:], in_=identity[:])
        pair_swap = keep.tile([P, P], F32)
        identity_pairs = identity[:].rearrange("p (j two) -> p j two", two=2)
        pair_swap_pairs = pair_swap[:].rearrange("p (j two) -> p j two", two=2)
        nc.vector.tensor_copy(out=pair_swap_pairs[:, :, 0:1], in_=identity_pairs[:, :, 1:2])
        nc.vector.tensor_copy(out=pair_swap_pairs[:, :, 1:2], in_=identity_pairs[:, :, 0:1])

        def load_weight(w, rows, heads):
            nc.sync.dma_start(
                out=rows[:].rearrange("p (h k) -> p h k", h=HEADS)[:, heads],
                in_=w.rearrange("(h p) k -> p h k", p=P)[:, heads],
            )

        def load_tokens(chunk, rows, blocks):
            b, place = divmod(chunk, CHUNKS_PER_BATCH)
            nc.sync.dma_start(
                out=rows[:].rearrange("p (i k) -> p i k", i=CHUNK_BLOCKS)[:, blocks],
                in_=hidden_states[b, place * CHUNK : (place + 1) * CHUNK, :].rearrange(
                    "(p i) k -> p i k", i=CHUNK_BLOCKS
                )[:, blocks],
            )

        def load_table(table, rows, places):
            nc.sync.dma_start(
                out=rows.rearrange("p c i d -> p c (i d)")[:, places],
                in_=table.rearrange("(c p i) d -> p c (i d)", p=P, i=CHUNK_BLOCKS)[:, places],
            )

        tables = keep.tile([P, 2, CHUNKS_PER_BATCH, CHUNK_BLOCKS, HEAD_DIM], BF16)
        flat_tables = keep.tile([P, 2, CHUNKS_PER_BATCH, CHUNK], BF16)
        sin_rows = keep.tile([P, CHUNKS_PER_BATCH, CHUNK_BLOCKS, HEAD_DIM], BF16)
        wq_rows = keep.tile([P, HEADS * EMBED], BF16)
        wk_rows = keep.tile([P, HEADS * EMBED], BF16)
        token_rows = []
        for chunk in range(CHUNKS):
            rows = tokens.tile([P, CHUNK_BLOCKS * EMBED], BF16, name="token_rows")
            token_rows.append(rows)
        halves = (slice(0, BANK_BLOCKS), slice(BANK_BLOCKS, 2 * BANK_BLOCKS))
        first_place, later_places = slice(0, 1), slice(1, CHUNKS_PER_BATCH)
        everything = slice(0, CHUNK_BLOCKS)
        for half in halves:
            load_weight(wq, wq_rows, half)
        load_tokens(0, token_rows[0], halves[0])
        load_table(sin, sin_rows[:], first_place)
        load_table(cos, tables[:, 0], first_place)
        load_tokens(0, token_rows[0], halves[1])
        load_weight(wk, wk_rows, everything)
        load_table(sin, sin_rows[:], later_places)
        load_tokens(1, token_rows[1], everything)
        load_table(cos, tables[:, 0], later_places)
        for chunk in range(2, CHUNKS):
            load_tokens(chunk, token_rows[chunk], everything)

        def turn_sin(place):
            given = sin_rows[:, place].rearrange("p i (j two) -> p (i j) two", two=2)
            made = tables[:, 1, place].rearrange("p i (j two) -> p (i j) two", two=2)
            for goes_to, comes_from, sign in ((1, 0, -1.0), (0, 1, 1.0)):
                nc.gpsimd.tensor_scalar(
                    out=made[:, :, goes_to : goes_to + 1],
                    in0=given[:, :, comes_from : comes_from + 1],
                    scalar1=sign,
                    scalar2=0.0,
                    op0=MULT,
                    op1=ADD,
                )

        def flatten_table(table, place):
            bank = flipped.tile([P, CHUNK], BF16, name="flipped_bank")
            for i in range(CHUNK_BLOCKS):
                nc.tensor.transpose(
                    bank[:, i * P : (i + 1) * P], tables[:, table, place, i, :], identity_bf16[:]
                )
            nc.scalar.copy(out=flat_tables[:, table, place, :], in_=bank[:])

        def regroup_bank(rows, grouped, first, copy, bank):
            words = rows[:].bitcast(F32)
            for j in range(BANK_BLOCKS):
                for u in range(2):
                    nc.tensor.transpose(
                        bank[:, (2 * j + u) * P : (2 * j + u + 1) * P],
                        words[:, (first + j) * WORDS + u : (first + j + 1) * WORDS : 2],
                        identity[:],
                    )
            grouped_words = grouped[:].bitcast(F32).rearrange("p (j r u) -> p j r u", r=P, u=2)
            copy(
                out=grouped_words[:, first : first + BANK_BLOCKS],
                in_=bank[:].rearrange("p (j u r) -> p j r u", j=BANK_BLOCKS, u=2),
            )

        def new_bank():
            return flipped.tile([P, BANK], F32, name="flipped_bank")

        def new_k_turn():
            return k_turns.tile([P, BANK], F32, name="k_turn")

        def new_grouped():
            return regroup.tile([P, GROUP * PACK], BF16, name="grouped", align_bytes=64)

        def new_operand(pool, tag, columns):
            codes = pool.tile([P, columns], U32, name=tag + "_codes", align_bytes=64)
            scales = pool.tile([P, columns], U8, name=tag + "_scales", align_bytes=64)
            return codes, scales

        def part_of(operand, columns):
            return operand[0][:, columns], operand[1][:, columns]

        def quantise(grouped, operand, columns):
            nc.vector.quantize_mx(
                out=operand[0][:, columns].bitcast(FP8X4),
                scales=operand[1][:, columns],
                in_=grouped[:, columns.start * PACK : columns.stop * PACK],
            )

        def multiply(bank, stationary, columns, moving):
            nc.tensor.matmul_mx(
                out=bank[:],
                lhsT=stationary[0][:, columns].bitcast(FP8X4),
                lhsT_scale=stationary[1][:, columns],
                rhs=moving[0][:].bitcast(FP8X4),
                rhs_scale=moving[1][:],
                start=True,
                stop=True,
            )

        def chunk_rows(out, chunk):
            b, place = divmod(chunk, CHUNKS_PER_BATCH)
            return out[b, :, place * CHUNK : (place + 1) * CHUNK, :].rearrange(
                "h (p i) d -> p h i d", i=CHUNK_BLOCKS
            )

        def q_multiply(step, operands, wq_operand):
            chunk, i = divmod(step, CHUNK_BLOCKS)
            bank = q_sums.tile([P, BANK], F32, name="q_bank")
            multiply(bank, operands[chunk], slice(i * P, (i + 1) * P), wq_operand)
            return bank

        def q_rotate(chunk, i, bank, products):
            both = [P, 2, HEADS, HEAD_DIM]
            nc.vector.tensor_tensor(
                out=products[:, :, :, i % PIECE_BLOCKS, :],
                in0=bank[:].rearrange("p (h d) -> p h d", h=HEADS).unsqueeze(1).to_broadcast(both),
                in1=tables[:, :, chunk % CHUNKS_PER_BATCH, i, :].unsqueeze(2).to_broadcast(both),
                op=MULT,
            )

        def q_add(blocks, products, adder):
            straight = products[:, 0, :, blocks].rearrange("p h i (j two) -> p h (i j) two", two=2)
            turned = products[:, 1, :, blocks].rearrange("p h i (j two) -> p h (i j) two", two=2)
            adder.tensor_tensor(out=straight, in0=straight, in1=turned[:, :, :, ::-1], op=ADD)

        def q_store(chunk, blocks, products):
            first = blocks.start % PIECE_BLOCKS
            part = products[:, 0, :, first : first + blocks.stop - blocks.start]
            nc.sync.dma_start(
                out=chunk_rows(out_0, chunk)[:, :, blocks, :].rearrange("p h i d -> p h (i d)"),
                in_=part.rearrange("p h i d -> p h (i d)"),
            )

        def k_multiply(chunk, h, token_operand, wk_operand, gpsimd_helps):
            bank = k_sums.tile([P, BANK], F32, name="k_bank")
            multiply(bank, wk_operand, slice(h * P, (h + 1) * P), token_operand)
            products = k_products.tile([P, 2, CHUNK], F32, name="k_pair")
            if gpsimd_helps:
                copied = k_copies.tile([P, CHUNK], F32, name="k_copied")
                nc.scalar.mul(out=copied[:], in_=bank[:], mul=K_FACTOR)
                nc.gpsimd.tensor_tensor(
                    out=products[:, 1],
                    in0=copied[:],
                    in1=flat_tables[:, 1, chunk % CHUNKS_PER_BATCH, :],
                    op=MULT,
                )
            return bank, products, 1 if gpsimd_helps else 2

        def k_rotate(chunk, bank, products, by_vector):
            nc.vector.scalar_tensor_tensor(
                out=products[:, 0:by_vector],
                in0=bank[:].unsqueeze(1).to_broadcast([P, by_vector, CHUNK]),
                scalar=K_FACTOR,
                in1=flat_tables[:, 0:by_vector, chunk % CHUNKS_PER_BATCH, :],
                op0=MULT,
                op1=MULT,
            )

        def k_finish(chunk, h, products):
            bank = new_k_turn()
            for i in range(CHUNK_BLOCKS):
                block = slice(i * P, (i + 1) * P)
                for table, permutation in ((0, identity), (1, pair_swap)):
                    nc.tensor.matmul(
                        out=bank[:, i * HEAD_DIM : (i + 1) * HEAD_DIM],
                        lhsT=products[:, table, block],
                        rhs=permutation[:],
                        is_transpose=True,
                        start=table == 0,
                        stop=table == 1,
                    )
            result = k_results.tile([P, CHUNK_BLOCKS * HEAD_DIM], F32, name="k_result")
            nc.scalar.copy(out=result[:], in_=bank[:])
            nc.sync.dma_start(
                out=chunk_rows(out_1, chunk)[:, h].rearrange("p i d -> p (i d)"),
                in_=result[:],
            )

        def heads_until(step):
            if step >= STEPS:
                return STEPS
            return max(0, (step - K_START) * (STEPS - 2) // (STEPS - 1 - K_START))

        def heads_of(step):
            return range(heads_until(step), heads_until(step + 1))

        with tc.manual_schedule():
            for place in range(CHUNKS_PER_BATCH):
                turn_sin(place)
            wq_grouped_tile, first_tile = new_grouped(), new_grouped()
            wk_grouped = keep.tile([P, CHUNK * PACK], BF16, align_bytes=64)
            wq_operand, wk_operand = new_operand(keep, "wq", CHUNK), new_operand(keep, "wk", CHUNK)
            whole = slice(0, CHUNK)
            first_operand = new_operand(quantised, "token", GROUP)
            operands = [part_of(first_operand, whole)]
            wq_grouped = wq_grouped_tile[:, 0 : CHUNK * PACK]
            grouped_first = first_tile[:, 0 : CHUNK * PACK]
            regroup_bank(wq_rows, wq_grouped, 0, nc.scalar.copy, new_k_turn())
            regroup_bank(wq_rows, wq_grouped, BANK_BLOCKS, nc.vector.tensor_copy, new_k_turn())
            for half in range(2):
                regroup_bank(token_rows[0], grouped_first, half * BANK_BLOCKS, nc.scalar.copy, new_bank())
            quantise(wq_grouped, wq_operand, whole)
            quantise(grouped_first, operands[0], slice(0, CHUNK // 2))
            q_banks, k_banks, q_results = {}, {}, {}
            gate = keep.tile([P, 1], U8)
            q_banks[0] = q_multiply(0, operands, wq_operand)
            for table in range(2):
                flatten_table(table, 0)
            bank_of, group_of = {}, {}
            for group in range(1, len(GROUPS)):
                quantise_step = GROUPS[group][0] * CHUNK_BLOCKS - 1
                group_of[quantise_step] = group
                banks = len(GROUPS[group]) * HALVES
                for bank in range(banks):
                    bank_of[quantise_step - banks + bank] = group, bank
            grouped_tokens = {}

            def fill_k_banks(k_steps, step):
                for k_step in k_steps:
                    chunk, h = divmod(k_step, CHUNK_BLOCKS)
                    gpsimd_helps = step % CHUNK_BLOCKS in GPSIMD_STEPS and k_step == heads_of(step)[0]
                    k_banks[k_step] = k_multiply(chunk, h, operands[chunk], wk_operand, gpsimd_helps)

            def store_q(step):
                chunk, i = divmod(step, CHUNK_BLOCKS)
                last = step >= STEPS - PIECE_BLOCKS
                if last:
                    q_store(chunk, slice(i, i + 1), q_results[step])
                elif i % PIECE_BLOCKS == PIECE_BLOCKS - 1:
                    q_store(chunk, slice(i + 1 - PIECE_BLOCKS, i + 1), q_results[step])

            for step in range(STEPS + SUM_LAG):
                chunk, i = divmod(step, CHUNK_BLOCKS)
                next_heads = heads_of(step + 1)
                if step > 1:
                    fill_k_banks(next_heads[:1], step + 1)
                if step != K_START:
                    for k_step in heads_of(step):
                        k_rotate(k_step // CHUNK_BLOCKS, *k_banks[k_step])
                if step < STEPS:
                    if i % PIECE_BLOCKS == 0:
                        products = q_products.tile(
                            [P, 2, HEADS, PIECE_BLOCKS, HEAD_DIM], F32, name="q_pair"
                        )
                    q_rotate(chunk, i, q_banks[step], products)
                    q_results[step] = products
                if step == K_START:
                    for k_step in heads_of(step):
                        k_rotate(k_step // CHUNK_BLOCKS, *k_banks[k_step])
                if step in group_of:
                    group = group_of[step]
                    operand = new_operand(quantised, "token", GROUP)
                    quantise(grouped_tokens[group], operand, slice(0, len(GROUPS[group]) * CHUNK))
                    for place in range(len(GROUPS[group])):
                        operands.append(part_of(operand, slice(place * CHUNK, (place + 1) * CHUNK)))
                    nc.gpsimd.tensor_copy(out=gate[:], in_=operand[1][:, 0:1])
                if step == 0:
                    quantise(grouped_first, operands[0], slice(CHUNK // 2, CHUNK))
                j = i % PIECE_BLOCKS
                if STEPS - PIECE_BLOCKS <= step < STEPS:
                    q_add(slice(j, j + 1), products, nc.vector if step == STEPS - 1 else nc.gpsimd)
                elif step < STEPS and j == PIECE_BLOCKS - 1:
                    q_add(slice(0, PIECE_BLOCKS), products, nc.gpsimd)
                if step not in group_of and step + 1 < STEPS:
                    q_banks[step + 1] = q_multiply(step + 1, operands, wq_operand)
                if step == 1:
                    quantise(wk_grouped, wk_operand, whole)
                    fill_k_banks(next_heads, step + 1)
                else:
                    fill_k_banks(next_heads[1:], step + 1)
                for k_step in heads_of(step - SUM_LAG):
                    k_finish(*divmod(k_step, CHUNK_BLOCKS), k_banks[k_step][1])
                if step == 0:
                    for half in range(2):
                        regroup_bank(wk_rows, wk_grouped, half * BANK_BLOCKS, nc.scalar.copy, new_bank())
                if chunk < CHUNKS_PER_BATCH - 1 and i >= 2:
                    flatten_table(i - 2, chunk + 1)
                if step in bank_of:
                    group, bank = bank_of[step]
                    if bank == 0:
                        grouped_tokens[group] = new_grouped()
                    place, half = divmod(bank, HALVES)
                    columns = slice(place * CHUNK * PACK, (place + 1) * CHUNK * PACK)
                    regroup_bank(
                        token_rows[GROUPS[group][place]],
                        grouped_tokens[group][:, columns],
                        half * BANK_BLOCKS,
                        nc.scalar.copy,
                        new_bank(),
                    )
                if step in group_of:
                    q_banks[step + 1] = q_multiply(step + 1, operands, wq_operand)
                if 0 < step <= STEPS:
                    store_q(step - 1)
